import numpy as np
import ml_dtypes


def mxq(x, axis, fmt="e4m3"):
    dtype, down = {"e4m3": (ml_dtypes.float8_e4m3fn, 7), "e5m2": (ml_dtypes.float8_e5m2, 14)}[fmt]
    v = np.moveaxis(np.asarray(x, np.float32).astype(ml_dtypes.bfloat16).astype(np.float64), axis, -1)
    blocks = v.reshape(v.shape[:-1] + (-1, 32))
    amax = np.abs(blocks).max(-1, keepdims=True)
    byte = np.maximum(np.where(amax > 0, np.frexp(amax)[1] - 1 + 127, 0) - down, 1)
    scale = np.exp2(byte - 127.0)
    codes = (blocks / scale).astype(np.float32).astype(dtype).astype(np.float64)
    return np.moveaxis((codes * scale).reshape(v.shape), -1, axis)


WIDE = False


def mx_kscale(k):
    if not WIDE:
        return np.ones(k)
    levels = np.array([10, -10, 5, -5, 0])
    if k % 512:
        return np.exp2(np.random.permutation(np.resize(levels, k // 32))).repeat(32)
    a = np.empty((k // 512, 16))
    for p in range(k // 512):
        a[p, :8] = np.random.permutation(np.resize(levels, 8))
        for g in range(8):
            far = levels[np.abs(levels - a[p, g]) >= 10]
            a[p, g + 8] = far[np.random.randint(len(far))]
    return np.exp2(a.ravel()).repeat(32)


BF16 = ml_dtypes.bfloat16


def bf(x):
    return np.asarray(x, np.float32).astype(BF16)


def f64(x):
    return np.asarray(x).astype(np.float64)


B, S, DIM, H, NOPE, ROPE, VD = 4, 1024, 1024, 4, 192, 64, 128
QK = NOPE + ROPE


def apply_rope(t, freqs):
    b, s, h, d = t.shape
    tr = t.reshape(b, s, h, d // 2, 2)
    cos = np.cos(freqs)[None, :, None, :]
    sin = np.sin(freqs)[None, :, None, :]
    out = np.stack([tr[..., 0] * cos - tr[..., 1] * sin,
                    tr[..., 0] * sin + tr[..., 1] * cos], axis=-1)
    return out.reshape(b, s, h, d)


def setup_inputs():
    s = mx_kscale(DIM)
    inv_freq = 1.0 / (10000.0 ** (np.arange(0, ROPE, 2) / ROPE))
    ang = np.arange(S)[:, None] * inv_freq[None, :]
    ang = ang - 2.0 * np.pi * np.round(ang / (2.0 * np.pi))
    return {"x": bf(np.random.standard_normal((B, S, DIM)) * s),
            "w": bf(np.random.standard_normal((DIM, H * QK)) / np.sqrt(DIM) / s[:, None]),
            "freqs": bf(ang)}


def reference(x, w, freqs):
    y = mxq(f64(x), 2, "e4m3") @ mxq(f64(w), 0, "e4m3")
    nope = y[..., :H * NOPE].reshape(B, S, H, NOPE)
    rope = apply_rope(y[..., H * NOPE:].reshape(B, S, H, ROPE), f64(freqs))
    return np.concatenate([nope, rope], axis=-1)

@@ -1,0 +1,257 @@
+from contextlib import ExitStack
+
+import concourse.mybir as mybir
+from concourse.masks import make_identity
+
+BF16 = mybir.dt.bfloat16
+F32 = mybir.dt.float32
+U32 = mybir.dt.uint32
+U8 = mybir.dt.uint8
+FP8X4 = mybir.dt.float8_e4m3fn_x4
+ACT = mybir.ActivationFunctionType
+ALU = mybir.AluOpType
+
+P = 128
+PACK = 4
+BATCH, SEQ, DIM = 4, 1024, 1024
+HEADS, NOPE, ROPE = 4, 192, 64
+QK = NOPE + ROPE
+PASSES = DIM // (P * PACK)
+TILES = SEQ // P
+PAIR = 2
+PAIRS_PER_BATCH = TILES // PAIR
+PAIRS = BATCH * PAIRS_PER_BATCH
+PART = 64
+CHUNKS = QK // PART
+CHUNK_COLS = HEADS * PART
+ROPE_CHUNK = CHUNKS - 1
+CHUNK_ORDER = (ROPE_CHUNK, 0, 1, 2)
+BANK = 512
+AHEAD = 2
+
+FLOPS = 2 * BATCH * SEQ * DIM * HEADS * QK
+
+
+def tile_mla_pa_t_kernel(tc, x, w, freqs, out):
+    nc = tc.nc
+    x_rows = x.rearrange("b (p i) k -> b p (i k)", i=TILES)
+    out_rows = out.rearrange("b (p i) h d -> b p (i h d)", i=TILES)
+
+    with ExitStack() as ctx:
+        const = ctx.enter_context(tc.tile_pool(name="const", bufs=1))
+        x_pool = ctx.enter_context(tc.tile_pool(name="x_pool", bufs=PAIRS))
+        grouped_pool = ctx.enter_context(tc.tile_pool(name="grouped_pool", bufs=3))
+        code_pool = ctx.enter_context(tc.tile_pool(name="code_pool", bufs=AHEAD + 2))
+        term_pool = ctx.enter_context(tc.tile_pool(name="term_pool", bufs=2))
+        out_pool = ctx.enter_context(tc.tile_pool(name="out_pool", bufs=6))
+        xt_pool = ctx.enter_context(tc.psum_pool(name="xt_pool", bufs=4))
+        acc_pool = ctx.enter_context(tc.psum_pool(name="acc_pool", bufs=4))
+        ctx.enter_context(tc.manual_schedule())
+
+        angles = const.tile([P, TILES * ROPE // 2], BF16)
+        nc.scalar.dma_start(out=angles[:], in_=freqs.rearrange("(p i) j -> p (i j)", i=TILES))
+
+        w_raw = const.tile([P, PASSES, PACK, DIM], BF16)
+
+        def load_w(g):
+            rows = w[g * P * PACK : (g + 1) * P * PACK, :]
+            nc.sync.dma_start(
+                out=w_raw[:, g].rearrange("p t n -> p (t n)"),
+                in_=rows.rearrange("(p t) n -> p (t n)", t=PACK),
+            )
+
+        x_tiles = {}
+
+        def load_x(r):
+            b, q = divmod(r, PAIRS_PER_BATCH)
+            x_sb = x_pool.tile([P, PAIR * DIM], BF16)
+            nc.sync.dma_start(out=x_sb[:], in_=x_rows[b, :, q * PAIR * DIM : (q + 1) * PAIR * DIM])
+            x_tiles[r] = x_sb
+
+        load_w(0)
+        load_x(0)
+        load_w(1)
+        for r in range(1, PAIRS):
+            load_x(r)
+
+        ident = const.tile([P, P], F32)
+        make_identity(nc, ident[:])
+
+        u_table = const.tile([P, TILES, ROPE], F32)
+        v_table = const.tile([P, TILES, ROPE], F32)
+        u_cols = u_table[:].rearrange("p i (j e) -> p (i j) e", e=2)
+        v_cols = v_table[:].rearrange("p i (j e) -> p (i j) e", e=2)
+        half_sin = const.tile([P, TILES * ROPE // 2], F32)
+        half_sq = const.tile([P, TILES * ROPE // 2], F32)
+        nc.scalar.activation(out=half_sin[:], in_=angles[:], func=ACT.Sin, scale=0.5)
+        nc.scalar.activation(out=u_cols[:, :, 1], in_=angles[:], func=ACT.Sin)
+        nc.scalar.activation(out=v_cols[:, :, 0], in_=angles[:], func=ACT.Sin, scale=-1.0)
+        nc.scalar.activation(out=half_sq[:], in_=half_sin[:], func=ACT.Square)
+        nc.scalar.activation(out=u_cols[:, :, 0], in_=half_sq[:], func=ACT.Copy, scale=-2.0, bias=1.0)
+        nc.scalar.activation(out=v_cols[:, :, 1], in_=half_sq[:], func=ACT.Copy, scale=-2.0, bias=1.0)
+
+        xt_banks = {}
+        grouped_tiles = {}
+        x_codes = {}
+        x_scales = {}
+
+        def transpose_pair(r):
+            words = x_tiles[r][:].bitcast(F32)
+            xt_banks[r] = []
+            for t in range(PAIR):
+                xt = xt_pool.tile([P, BANK], F32)
+                for s in range(PACK):
+                    g, u = divmod(s, 2)
+                    first = t * BANK + g * 2 * P
+                    nc.tensor.transpose(
+                        out=xt[:, s * P : (s + 1) * P],
+                        in_=words[:, first + u : first + 2 * P : 2],
+                        identity=ident[:],
+                    )
+                xt_banks[r].append(xt)
+
+        def group_pair(r):
+            grouped = grouped_pool.tile([P, PAIR * DIM], BF16, align_bytes=64)
+            grouped_words = grouped[:].bitcast(F32)
+            for t in range(PAIR):
+                nc.scalar.copy(
+                    out=grouped_words[:, t * BANK : (t + 1) * BANK].rearrange(
+                        "p (g k u) -> p g k u", g=PASSES, u=2
+                    ),
+                    in_=xt_banks[r][t][:].rearrange("p (g u k) -> p g k u", g=PASSES, u=2),
+                )
+            grouped_tiles[r] = grouped
+
+        def quantise_pair(r):
+            codes = code_pool.tile([P, PAIR * PASSES * P], U32, align_bytes=64)
+            scales = code_pool.tile([P, PAIR * PASSES * P], U8, align_bytes=64)
+            nc.vector.quantize_mx(
+                out=codes[:].bitcast(FP8X4), scales=scales[:], in_=grouped_tiles[r][:]
+            )
+            x_codes[r] = codes
+            x_scales[r] = scales
+
+        w_grouped = const.tile([P, PASSES, CHUNKS, CHUNK_COLS * PACK], BF16, align_bytes=64)
+        w_codes = const.tile([P, PASSES, CHUNKS * CHUNK_COLS], U32, align_bytes=64)
+        w_scales = const.tile([P, PASSES, CHUNKS * CHUNK_COLS], U8, align_bytes=64)
+
+        def group_w(g, c, on_scalar):
+            if c == ROPE_CHUNK:
+                src = w_raw[:, g, :, HEADS * NOPE :].rearrange("p t (h n) -> p h n t", h=HEADS)
+            else:
+                src = w_raw[:, g, :, : HEADS * NOPE].rearrange(
+                    "p t (h c n) -> p c h n t", h=HEADS, n=PART
+                )[:, c]
+            dst = w_grouped[:, g, c, :].rearrange("p (h n t) -> p h n t", h=HEADS, t=PACK)
+            if on_scalar:
+                nc.scalar.copy(out=dst, in_=src)
+            else:
+                nc.vector.tensor_copy(out=dst, in_=src)
+
+        def quantise_w(g, c):
+            cols = slice(c * CHUNK_COLS, (c + 1) * CHUNK_COLS)
+            nc.vector.quantize_mx(
+                out=w_codes[:, g, cols].bitcast(FP8X4),
+                scales=w_scales[:, g, cols],
+                in_=w_grouped[:, g, c, :],
+            )
+
+        def prepare_w(g, share_with_scalar):
+            for n, c in enumerate(CHUNK_ORDER):
+                group_w(g, c, on_scalar=share_with_scalar and n % 2 == 1)
+                if n > 0:
+                    quantise_w(g, CHUNK_ORDER[n - 1])
+            quantise_w(g, CHUNK_ORDER[-1])
+
+        acc_banks = {}
+        out_tiles = {}
+
+        def multiply_pair(r):
+            for c in CHUNK_ORDER:
+                acc = acc_pool.tile([P, BANK], F32)
+                w_cols = slice(c * CHUNK_COLS, (c + 1) * CHUNK_COLS)
+                for t in range(PAIR):
+                    for g in range(PASSES):
+                        x_cols = slice((t * PASSES + g) * P, (t * PASSES + g + 1) * P)
+                        nc.tensor.matmul_mx(
+                            out=acc[:, t * CHUNK_COLS : (t + 1) * CHUNK_COLS],
+                            lhsT=x_codes[r][:, x_cols].bitcast(FP8X4),
+                            lhsT_scale=x_scales[r][:, x_cols],
+                            rhs=w_codes[:, g, w_cols].bitcast(FP8X4),
+                            rhs_scale=w_scales[:, g, w_cols],
+                            start=(g == 0),
+                            stop=(g == PASSES - 1),
+                        )
+                acc_banks[r, c] = acc
+
+        full = [P, PAIR, HEADS, ROPE // 2, 2]
+        split = "p (t h j e) -> p t h j e"
+
+        def rotate_products(r):
+            i0 = (r % PAIRS_PER_BATCH) * PAIR
+            pairs = acc_banks[r, ROPE_CHUNK][:].rearrange(split, t=PAIR, h=HEADS, e=2)
+            terms = []
+            for e, table in enumerate((u_table, v_table)):
+                term = term_pool.tile([P, BANK], F32, name="term%d" % e)
+                nc.vector.tensor_tensor(
+                    out=term[:].rearrange(split, t=PAIR, h=HEADS, e=2),
+                    in0=pairs[:, :, :, :, e : e + 1].to_broadcast(full),
+                    in1=table[:, i0 : i0 + PAIR, :]
+                    .rearrange("p t (j e) -> p t j e", e=2)
+                    .unsqueeze(2)
+                    .to_broadcast(full),
+                    op=ALU.mult,
+                )
+                terms.append(term)
+            return terms
+
+        def out_part(r, c):
+            view = out_tiles[r][:].rearrange("p (t h d) -> p t h d", t=PAIR, h=HEADS)
+            return view[:, :, :, c * PART : (c + 1) * PART]
+
+        by_head = "p (t h n) -> p t h n"
+
+        def rotate_sum(r, terms):
+            nc.vector.tensor_tensor(
+                out=out_part(r, ROPE_CHUNK),
+                in0=terms[0][:].rearrange(by_head, t=PAIR, h=HEADS),
+                in1=terms[1][:].rearrange(by_head, t=PAIR, h=HEADS),
+                op=ALU.add,
+            )
+
+        def copy_nope(r):
+            for c in range(ROPE_CHUNK):
+                nc.scalar.copy(
+                    out=out_part(r, c),
+                    in_=acc_banks[r, c][:].rearrange(by_head, t=PAIR, h=HEADS),
+                )
+
+        def store_pair(r):
+            b, q = divmod(r, PAIRS_PER_BATCH)
+            width = PAIR * HEADS * QK
+            nc.sync.dma_start(out=out_rows[b, :, q * width : (q + 1) * width], in_=out_tiles[r][:])
+
+        transpose_pair(0)
+        group_pair(0)
+        prepare_w(0, share_with_scalar=False)
+        quantise_pair(0)
+        prepare_w(1, share_with_scalar=True)
+        transpose_pair(1)
+        group_pair(1)
+        quantise_pair(1)
+
+        for r in range(PAIRS):
+            ahead = r + AHEAD
+            if ahead < PAIRS:
+                transpose_pair(ahead)
+            multiply_pair(r)
+            if ahead < PAIRS:
+                group_pair(ahead)
+            out_sb = out_pool.tile([P, PAIR * HEADS * QK], F32)
+            out_tiles[r] = out_sb
+            terms = rotate_products(r)
+            if ahead < PAIRS:
+                quantise_pair(ahead)
+            rotate_sum(r, terms)
+            copy_nope(r)
+            store_pair(r)

@@ -40,6 +40,7 @@ def tile_mla_pa_t_kernel(tc, x, w, freqs, out):
     with ExitStack() as ctx:
         const = ctx.enter_context(tc.tile_pool(name="const", bufs=1))
         x_pool = ctx.enter_context(tc.tile_pool(name="x_pool", bufs=PAIRS))
+        perm_pool = ctx.enter_context(tc.tile_pool(name="perm_pool", bufs=3))
         grouped_pool = ctx.enter_context(tc.tile_pool(name="grouped_pool", bufs=3))
         code_pool = ctx.enter_context(tc.tile_pool(name="code_pool", bufs=AHEAD + 2))
         term_pool = ctx.enter_context(tc.tile_pool(name="term_pool", bufs=2))
@@ -90,23 +91,29 @@ def tile_mla_pa_t_kernel(tc, x, w, freqs, out):
         nc.scalar.activation(out=u_cols[:, :, 0], in_=half_sq[:], func=ACT.Copy, scale=-2.0, bias=1.0)
         nc.scalar.activation(out=v_cols[:, :, 1], in_=half_sq[:], func=ACT.Copy, scale=-2.0, bias=1.0)
 
+        split_tiles = {}
         xt_banks = {}
         grouped_tiles = {}
         x_codes = {}
         x_scales = {}
 
+        def split_pair(r):
+            split = perm_pool.tile([P, PAIR * DIM], BF16)
+            nc.vector.tensor_copy(
+                out=split[:].bitcast(F32).rearrange("p (s u m) -> p s u m", u=2, m=P),
+                in_=x_tiles[r][:].bitcast(F32).rearrange("p (s m u) -> p s u m", u=2, m=P),
+            )
+            split_tiles[r] = split
+
         def transpose_pair(r):
-            words = x_tiles[r][:].bitcast(F32)
+            words = split_tiles[r][:].bitcast(F32)
             xt_banks[r] = []
             for t in range(PAIR):
                 xt = xt_pool.tile([P, BANK], F32)
                 for s in range(PACK):
-                    g, u = divmod(s, 2)
-                    first = t * BANK + g * 2 * P
+                    col = (t * PACK + s) * P
                     nc.tensor.transpose(
-                        out=xt[:, s * P : (s + 1) * P],
-                        in_=words[:, first + u : first + 2 * P : 2],
-                        identity=ident[:],
+                        out=xt[:, s * P : (s + 1) * P], in_=words[:, col : col + P], identity=ident[:]
                     )
                 xt_banks[r].append(xt)
 
@@ -231,11 +238,14 @@ def tile_mla_pa_t_kernel(tc, x, w, freqs, out):
             width = PAIR * HEADS * QK
             nc.sync.dma_start(out=out_rows[b, :, q * width : (q + 1) * width], in_=out_tiles[r][:])
 
+        split_pair(0)
         transpose_pair(0)
         group_pair(0)
         prepare_w(0, share_with_scalar=False)
         quantise_pair(0)
+        split_pair(1)
         prepare_w(1, share_with_scalar=True)
+        split_pair(2)
         transpose_pair(1)
         group_pair(1)
         quantise_pair(1)
@@ -253,5 +263,7 @@ def tile_mla_pa_t_kernel(tc, x, w, freqs, out):
             if ahead < PAIRS:
                 quantise_pair(ahead)
             rotate_sum(r, terms)
+            if ahead + 1 < PAIRS:
+                split_pair(ahead + 1)
             copy_nope(r)
             store_pair(r)

@@ -28,6 +28,8 @@ ROPE_CHUNK = CHUNKS - 1
 CHUNK_ORDER = (ROPE_CHUNK, 0, 1, 2)
 BANK = 512
 AHEAD = 2
+TILEWISE = (0, PAIRS - 1)
+HEAD = 3
 
 FLOPS = 2 * BATCH * SEQ * DIM * HEADS * QK
 
@@ -50,7 +52,7 @@ def tile_mla_pa_t_kernel(tc, x, w, freqs, out):
         ctx.enter_context(tc.manual_schedule())
 
         angles = const.tile([P, TILES * ROPE // 2], BF16)
-        nc.scalar.dma_start(out=angles[:], in_=freqs.rearrange("(p i) j -> p (i j)", i=TILES))
+        nc.sync.dma_start(out=angles[:], in_=freqs.rearrange("(p i) j -> p (i j)", i=TILES))
 
         w_raw = const.tile([P, PASSES, PACK, DIM], BF16)
 
@@ -69,8 +71,8 @@ def tile_mla_pa_t_kernel(tc, x, w, freqs, out):
             nc.sync.dma_start(out=x_sb[:], in_=x_rows[b, :, q * PAIR * DIM : (q + 1) * PAIR * DIM])
             x_tiles[r] = x_sb
 
-        load_w(0)
         load_x(0)
+        load_w(0)
         load_w(1)
         for r in range(1, PAIRS):
             load_x(r)
@@ -87,9 +89,11 @@ def tile_mla_pa_t_kernel(tc, x, w, freqs, out):
         nc.scalar.activation(out=half_sin[:], in_=angles[:], func=ACT.Sin, scale=0.5)
         nc.scalar.activation(out=u_cols[:, :, 1], in_=angles[:], func=ACT.Sin)
         nc.scalar.activation(out=v_cols[:, :, 0], in_=angles[:], func=ACT.Sin, scale=-1.0)
-        nc.scalar.activation(out=half_sq[:], in_=half_sin[:], func=ACT.Square)
-        nc.scalar.activation(out=u_cols[:, :, 0], in_=half_sq[:], func=ACT.Copy, scale=-2.0, bias=1.0)
-        nc.scalar.activation(out=v_cols[:, :, 1], in_=half_sq[:], func=ACT.Copy, scale=-2.0, bias=1.0)
+        nc.vector.tensor_tensor(out=half_sq[:], in0=half_sin[:], in1=half_sin[:], op=ALU.mult)
+        for cos_cols in (u_cols[:, :, 0], v_cols[:, :, 1]):
+            nc.vector.tensor_scalar(
+                out=cos_cols, in0=half_sq[:], scalar1=-2.0, scalar2=1.0, op0=ALU.mult, op1=ALU.add
+            )
 
         split_tiles = {}
         xt_banks = {}
@@ -106,14 +110,20 @@ def tile_mla_pa_t_kernel(tc, x, w, freqs, out):
             split_tiles[r] = split
 
         def transpose_pair(r):
-            words = split_tiles[r][:].bitcast(F32)
+            words = (x_tiles[r] if r < HEAD else split_tiles[r])[:].bitcast(F32)
             xt_banks[r] = []
             for t in range(PAIR):
                 xt = xt_pool.tile([P, BANK], F32)
                 for s in range(PACK):
-                    col = (t * PACK + s) * P
+                    g, u = divmod(s, 2)
+                    if r < HEAD:
+                        first = t * BANK + g * 2 * P
+                        cols = slice(first + u, first + 2 * P, 2)
+                    else:
+                        first = (t * PACK + s) * P
+                        cols = slice(first, first + P)
                     nc.tensor.transpose(
-                        out=xt[:, s * P : (s + 1) * P], in_=words[:, col : col + P], identity=ident[:]
+                        out=xt[:, s * P : (s + 1) * P], in_=words[:, cols], identity=ident[:]
                     )
                 xt_banks[r].append(xt)
 
@@ -155,55 +165,68 @@ def tile_mla_pa_t_kernel(tc, x, w, freqs, out):
             else:
                 nc.vector.tensor_copy(out=dst, in_=src)
 
-        def quantise_w(g, c):
-            cols = slice(c * CHUNK_COLS, (c + 1) * CHUNK_COLS)
+        def quantise_w_half(g, half):
+            cols = slice(half * BANK, (half + 1) * BANK)
             nc.vector.quantize_mx(
                 out=w_codes[:, g, cols].bitcast(FP8X4),
                 scales=w_scales[:, g, cols],
-                in_=w_grouped[:, g, c, :],
+                in_=w_grouped[:, g, 2 * half : 2 * half + 2, :].rearrange("p c k -> p (c k)"),
             )
-
-        def prepare_w(g, share_with_scalar):
-            for n, c in enumerate(CHUNK_ORDER):
-                group_w(g, c, on_scalar=share_with_scalar and n % 2 == 1)
-                if n > 0:
-                    quantise_w(g, CHUNK_ORDER[n - 1])
-            quantise_w(g, CHUNK_ORDER[-1])
 
         acc_banks = {}
         out_tiles = {}
 
+        def multiply(acc_cols, r, t, w_cols, passes):
+            for g in passes:
+                x_cols = slice((t * PASSES + g) * P, (t * PASSES + g + 1) * P)
+                nc.tensor.matmul_mx(
+                    out=acc_cols,
+                    lhsT=x_codes[r][:, x_cols].bitcast(FP8X4),
+                    lhsT_scale=x_scales[r][:, x_cols],
+                    rhs=w_codes[:, g, w_cols].bitcast(FP8X4),
+                    rhs_scale=w_scales[:, g, w_cols],
+                    start=(g == 0),
+                    stop=(g == PASSES - 1),
+                )
+
         def multiply_pair(r):
             for c in CHUNK_ORDER:
                 acc = acc_pool.tile([P, BANK], F32)
-                w_cols = slice(c * CHUNK_COLS, (c + 1) * CHUNK_COLS)
-                for t in range(PAIR):
-                    for g in range(PASSES):
-                        x_cols = slice((t * PASSES + g) * P, (t * PASSES + g + 1) * P)
-                        nc.tensor.matmul_mx(
-                            out=acc[:, t * CHUNK_COLS : (t + 1) * CHUNK_COLS],
-                            lhsT=x_codes[r][:, x_cols].bitcast(FP8X4),
-                            lhsT_scale=x_scales[r][:, x_cols],
-                            rhs=w_codes[:, g, w_cols].bitcast(FP8X4),
-                            rhs_scale=w_scales[:, g, w_cols],
-                            start=(g == 0),
-                            stop=(g == PASSES - 1),
-                        )
                 acc_banks[r, c] = acc
+                for t in range(PAIR):
+                    multiply(
+                        acc[:, t * CHUNK_COLS : (t + 1) * CHUNK_COLS],
+                        r, t, slice(c * CHUNK_COLS, (c + 1) * CHUNK_COLS), range(PASSES),
+                    )
 
-        full = [P, PAIR, HEADS, ROPE // 2, 2]
+        def multiply_half(r, t, half, passes):
+            if 0 in passes:
+                acc = acc_pool.tile([P, BANK], F32)
+                acc_banks[r, t, half] = acc
+            multiply(acc_banks[r, t, half][:], r, t, slice(half * BANK, (half + 1) * BANK), passes)
+
+        def bank_part(r, tiles, c):
+            if r in TILEWISE:
+                half, side = divmod(c, 2)
+                return acc_banks[r, tiles.start, half][:, side * CHUNK_COLS : (side + 1) * CHUNK_COLS]
+            return acc_banks[r, c][:]
+
         split = "p (t h j e) -> p t h j e"
+        by_head = "p (t h n) -> p t h n"
+        both = slice(0, PAIR)
 
-        def rotate_products(r):
-            i0 = (r % PAIRS_PER_BATCH) * PAIR
-            pairs = acc_banks[r, ROPE_CHUNK][:].rearrange(split, t=PAIR, h=HEADS, e=2)
+        def rotate_products(r, tiles=both):
+            count = tiles.stop - tiles.start
+            full = [P, count, HEADS, ROPE // 2, 2]
+            i0 = (r % PAIRS_PER_BATCH) * PAIR + tiles.start
+            pairs = bank_part(r, tiles, ROPE_CHUNK).rearrange(split, t=count, h=HEADS, e=2)
             terms = []
             for e, table in enumerate((u_table, v_table)):
                 term = term_pool.tile([P, BANK], F32, name="term%d" % e)
                 nc.vector.tensor_tensor(
-                    out=term[:].rearrange(split, t=PAIR, h=HEADS, e=2),
+                    out=term[:, : count * CHUNK_COLS].rearrange(split, t=count, h=HEADS, e=2),
                     in0=pairs[:, :, :, :, e : e + 1].to_broadcast(full),
-                    in1=table[:, i0 : i0 + PAIR, :]
+                    in1=table[:, i0 : i0 + count, :]
                     .rearrange("p t (j e) -> p t j e", e=2)
                     .unsqueeze(2)
                     .to_broadcast(full),
@@ -212,49 +235,100 @@ def tile_mla_pa_t_kernel(tc, x, w, freqs, out):
                 terms.append(term)
             return terms
 
-        def out_part(r, c):
-            view = out_tiles[r][:].rearrange("p (t h d) -> p t h d", t=PAIR, h=HEADS)
-            return view[:, :, :, c * PART : (c + 1) * PART]
+        def out_view(r, tiles):
+            return out_tiles[r][:].rearrange("p (t h d) -> p t h d", t=PAIR, h=HEADS)[:, tiles]
 
-        by_head = "p (t h n) -> p t h n"
+        def out_part(r, tiles, c):
+            return out_view(r, tiles)[:, :, :, c * PART : (c + 1) * PART]
 
-        def rotate_sum(r, terms):
+        def rotate_sum(r, terms, tiles=both):
+            count = tiles.stop - tiles.start
+            in0, in1 = (
+                term[:, : count * CHUNK_COLS].rearrange(by_head, t=count, h=HEADS) for term in terms
+            )
             nc.vector.tensor_tensor(
-                out=out_part(r, ROPE_CHUNK),
-                in0=terms[0][:].rearrange(by_head, t=PAIR, h=HEADS),
-                in1=terms[1][:].rearrange(by_head, t=PAIR, h=HEADS),
-                op=ALU.add,
+                out=out_part(r, tiles, ROPE_CHUNK), in0=in0, in1=in1, op=ALU.add
             )
 
         def copy_nope(r):
             for c in range(ROPE_CHUNK):
                 nc.scalar.copy(
-                    out=out_part(r, c),
-                    in_=acc_banks[r, c][:].rearrange(by_head, t=PAIR, h=HEADS),
+                    out=out_part(r, both, c),
+                    in_=bank_part(r, both, c).rearrange(by_head, t=PAIR, h=HEADS),
                 )
 
-        def store_pair(r):
-            b, q = divmod(r, PAIRS_PER_BATCH)
-            width = PAIR * HEADS * QK
-            nc.sync.dma_start(out=out_rows[b, :, q * width : (q + 1) * width], in_=out_tiles[r][:])
+        def copy_half0(r, t):
+            nc.scalar.copy(
+                out=out_view(r, slice(t, t + 1))[:, 0, :, : 2 * PART].rearrange(
+                    "p h (c n) -> p c h n", c=2
+                ),
+                in_=acc_banks[r, t, 0][:].rearrange("p (c h n) -> p c h n", c=2, h=HEADS),
+            )
 
-        split_pair(0)
+        def copy_chunk2(r, t, on_scalar):
+            tile = slice(t, t + 1)
+            dst = out_part(r, tile, 2)
+            src = bank_part(r, tile, 2).rearrange(by_head, t=1, h=HEADS)
+            if on_scalar:
+                nc.scalar.copy(out=dst, in_=src)
+            else:
+                nc.vector.tensor_copy(out=dst, in_=src)
+
+        def store(r, tiles=both):
+            b, q = divmod(r, PAIRS_PER_BATCH)
+            width = HEADS * QK
+            nc.sync.dma_start(
+                out=out_rows[b, :, (q * PAIR + tiles.start) * width : (q * PAIR + tiles.stop) * width],
+                in_=out_tiles[r][:, tiles.start * width : tiles.stop * width],
+            )
+
+        rope, nope0, nope1, nope2 = CHUNK_ORDER
+        tile_slices = [slice(t, t + 1) for t in range(PAIR)]
         transpose_pair(0)
         group_pair(0)
-        prepare_w(0, share_with_scalar=False)
+        for g in range(PASSES):
+            group_w(g, nope2, on_scalar=True)
+            group_w(g, nope0, on_scalar=True)
+        group_w(0, rope, on_scalar=False)
+        group_w(0, nope1, on_scalar=False)
         quantise_pair(0)
-        split_pair(1)
-        prepare_w(1, share_with_scalar=True)
-        split_pair(2)
+        quantise_w_half(0, 1)
+        quantise_w_half(0, 0)
+        for half in (1, 0):
+            for t in range(PAIR):
+                multiply_half(0, t, half, (0,))
         transpose_pair(1)
+        group_w(1, rope, on_scalar=False)
+        quantise_w_half(1, 1)
+        group_w(1, nope1, on_scalar=False)
+        quantise_w_half(1, 0)
+        for half in (1, 0):
+            for t in range(PAIR):
+                multiply_half(0, t, half, (1,))
+        transpose_pair(2)
         group_pair(1)
+        split_pair(HEAD)
         quantise_pair(1)
+        out_sb = out_pool.tile([P, PAIR * HEADS * QK], F32)
+        out_tiles[0] = out_sb
+        for t in range(PAIR):
+            copy_chunk2(0, t, on_scalar=True)
+            copy_half0(0, t)
+        group_pair(2)
+        for tile in tile_slices:
+            rotate_sum(0, rotate_products(0, tile), tile)
+        split_pair(HEAD + 1)
+        quantise_pair(2)
+        store(0)
 
-        for r in range(PAIRS):
+        for r in range(1, PAIRS - 1):
             ahead = r + AHEAD
-            if ahead < PAIRS:
-                transpose_pair(ahead)
+            if ahead + 2 < PAIRS:
+                split_pair(ahead + 2)
             multiply_pair(r)
+            for n in (ahead, ahead + 1) if r == 1 else (ahead + 1,):
+                if n < PAIRS:
+                    transpose_pair(n)
             if ahead < PAIRS:
                 group_pair(ahead)
             out_sb = out_pool.tile([P, PAIR * HEADS * QK], F32)
@@ -263,7 +337,16 @@ def tile_mla_pa_t_kernel(tc, x, w, freqs, out):
             if ahead < PAIRS:
                 quantise_pair(ahead)
             rotate_sum(r, terms)
-            if ahead + 1 < PAIRS:
-                split_pair(ahead + 1)
             copy_nope(r)
-            store_pair(r)
+            store(r)
+
+        last = PAIRS - 1
+        out_sb = out_pool.tile([P, PAIR * HEADS * QK], F32)
+        out_tiles[last] = out_sb
+        for t, tile in enumerate(tile_slices):
+            for half in (1, 0):
+                multiply_half(last, t, half, range(PASSES))
+            rotate_sum(last, rotate_products(last, tile), tile)
+            copy_chunk2(last, t, on_scalar=False)
+            copy_half0(last, t)
+            store(last, tile)

@@ -28,8 +28,9 @@ ROPE_CHUNK = CHUNKS - 1
 CHUNK_ORDER = (ROPE_CHUNK, 0, 1, 2)
 BANK = 512
 AHEAD = 2
-TILEWISE = (0, PAIRS - 1)
-HEAD = 3
+LAST = PAIRS - 1
+TILEWISE = (0, LAST)
+HEAD = 4
 
 FLOPS = 2 * BATCH * SEQ * DIM * HEADS * QK
 
@@ -174,6 +175,7 @@ def tile_mla_pa_t_kernel(tc, x, w, freqs, out):
             )
 
         acc_banks = {}
+        acc_parts = {}
         out_tiles = {}
 
         def multiply(acc_cols, r, t, w_cols, passes):
@@ -205,7 +207,15 @@ def tile_mla_pa_t_kernel(tc, x, w, freqs, out):
                 acc_banks[r, t, half] = acc
             multiply(acc_banks[r, t, half][:], r, t, slice(half * BANK, (half + 1) * BANK), passes)
 
+        def multiply_chunk(r, t, c):
+            xt = xt_pool.tile([P, BANK], F32)
+            acc_parts[r, t, c] = xt
+            cols = slice(c * CHUNK_COLS, (c + 1) * CHUNK_COLS)
+            multiply(xt[:, :CHUNK_COLS], r, t, cols, range(PASSES))
+
         def bank_part(r, tiles, c):
+            if (r, tiles.start, c) in acc_parts:
+                return acc_parts[r, tiles.start, c][:, :CHUNK_COLS]
             if r in TILEWISE:
                 half, side = divmod(c, 2)
                 return acc_banks[r, tiles.start, half][:, side * CHUNK_COLS : (side + 1) * CHUNK_COLS]
@@ -241,14 +251,12 @@ def tile_mla_pa_t_kernel(tc, x, w, freqs, out):
         def out_part(r, tiles, c):
             return out_view(r, tiles)[:, :, :, c * PART : (c + 1) * PART]
 
-        def rotate_sum(r, terms, tiles=both):
+        def rotate_sum(r, terms, tiles=both, engine=nc.vector):
             count = tiles.stop - tiles.start
             in0, in1 = (
                 term[:, : count * CHUNK_COLS].rearrange(by_head, t=count, h=HEADS) for term in terms
             )
-            nc.vector.tensor_tensor(
-                out=out_part(r, tiles, ROPE_CHUNK), in0=in0, in1=in1, op=ALU.add
-            )
+            engine.tensor_tensor(out=out_part(r, tiles, ROPE_CHUNK), in0=in0, in1=in1, op=ALU.add)
 
         def copy_nope(r):
             for c in range(ROPE_CHUNK):
@@ -265,14 +273,12 @@ def tile_mla_pa_t_kernel(tc, x, w, freqs, out):
                 in_=acc_banks[r, t, 0][:].rearrange("p (c h n) -> p c h n", c=2, h=HEADS),
             )
 
-        def copy_chunk2(r, t, on_scalar):
+        def copy_chunk2(r, t):
             tile = slice(t, t + 1)
-            dst = out_part(r, tile, 2)
-            src = bank_part(r, tile, 2).rearrange(by_head, t=1, h=HEADS)
-            if on_scalar:
-                nc.scalar.copy(out=dst, in_=src)
-            else:
-                nc.vector.tensor_copy(out=dst, in_=src)
+            nc.scalar.copy(
+                out=out_part(r, tile, 2),
+                in_=bank_part(r, tile, 2).rearrange(by_head, t=1, h=HEADS),
+            )
 
         def store(r, tiles=both):
             b, q = divmod(r, PAIRS_PER_BATCH)
@@ -306,29 +312,30 @@ def tile_mla_pa_t_kernel(tc, x, w, freqs, out):
             for t in range(PAIR):
                 multiply_half(0, t, half, (1,))
         transpose_pair(2)
+        transpose_pair(3)
         group_pair(1)
-        split_pair(HEAD)
         quantise_pair(1)
         out_sb = out_pool.tile([P, PAIR * HEADS * QK], F32)
         out_tiles[0] = out_sb
         for t in range(PAIR):
-            copy_chunk2(0, t, on_scalar=True)
+            copy_chunk2(0, t)
             copy_half0(0, t)
         group_pair(2)
         for tile in tile_slices:
-            rotate_sum(0, rotate_products(0, tile), tile)
-        split_pair(HEAD + 1)
+            rotate_sum(0, rotate_products(0, tile), tile, engine=nc.gpsimd)
+        split_pair(HEAD)
         quantise_pair(2)
         store(0)
 
-        for r in range(1, PAIRS - 1):
+        for r in range(1, LAST):
             ahead = r + AHEAD
-            if ahead + 2 < PAIRS:
-                split_pair(ahead + 2)
+            if r + HEAD < PAIRS:
+                split_pair(r + HEAD)
+            if r % 2 == 0:
+                for n in (ahead, ahead + 1):
+                    if n < PAIRS:
+                        transpose_pair(n)
             multiply_pair(r)
-            for n in (ahead, ahead + 1) if r == 1 else (ahead + 1,):
-                if n < PAIRS:
-                    transpose_pair(n)
             if ahead < PAIRS:
                 group_pair(ahead)
             out_sb = out_pool.tile([P, PAIR * HEADS * QK], F32)
@@ -340,13 +347,13 @@ def tile_mla_pa_t_kernel(tc, x, w, freqs, out):
             copy_nope(r)
             store(r)
 
-        last = PAIRS - 1
         out_sb = out_pool.tile([P, PAIR * HEADS * QK], F32)
-        out_tiles[last] = out_sb
+        out_tiles[LAST] = out_sb
         for t, tile in enumerate(tile_slices):
-            for half in (1, 0):
-                multiply_half(last, t, half, range(PASSES))
-            rotate_sum(last, rotate_products(last, tile), tile)
-            copy_chunk2(last, t, on_scalar=False)
-            copy_half0(last, t)
-            store(last, tile)
+            multiply_chunk(LAST, t, rope)
+            multiply_chunk(LAST, t, nope2)
+            multiply_half(LAST, t, 0, range(PASSES))
+            rotate_sum(LAST, rotate_products(LAST, tile), tile)
+            copy_chunk2(LAST, t)
+            copy_half0(LAST, t)
+            store(LAST, tile)

@@ -29,6 +29,8 @@ CHUNK_ORDER = (ROPE_CHUNK, 0, 1, 2)
 BANK = 512
 AHEAD = 2
 LAST = PAIRS - 1
+WARM_EARLY = 7
+WARM_LATE = 6
 TILEWISE = (0, LAST)
 HEAD = 4
 
@@ -46,7 +48,7 @@ def tile_mla_pa_t_kernel(tc, x, w, freqs, out):
         perm_pool = ctx.enter_context(tc.tile_pool(name="perm_pool", bufs=3))
         grouped_pool = ctx.enter_context(tc.tile_pool(name="grouped_pool", bufs=3))
         code_pool = ctx.enter_context(tc.tile_pool(name="code_pool", bufs=AHEAD + 2))
-        term_pool = ctx.enter_context(tc.tile_pool(name="term_pool", bufs=2))
+        term_pool = ctx.enter_context(tc.tile_pool(name="term_pool", bufs=3))
         out_pool = ctx.enter_context(tc.tile_pool(name="out_pool", bufs=6))
         xt_pool = ctx.enter_context(tc.psum_pool(name="xt_pool", bufs=4))
         acc_pool = ctx.enter_context(tc.psum_pool(name="acc_pool", bufs=4))
@@ -72,12 +74,14 @@ def tile_mla_pa_t_kernel(tc, x, w, freqs, out):
             nc.sync.dma_start(out=x_sb[:], in_=x_rows[b, :, q * PAIR * DIM : (q + 1) * PAIR * DIM])
             x_tiles[r] = x_sb
 
-        load_x(0)
         load_w(0)
+        load_x(0)
         load_w(1)
         for r in range(1, PAIRS):
             load_x(r)
 
+        zeros = const.tile([P, BANK], BF16)
+        nc.gpsimd.memset(zeros[:], 0.0)
         ident = const.tile([P, P], F32)
         make_identity(nc, ident[:])
 
@@ -173,6 +177,11 @@ def tile_mla_pa_t_kernel(tc, x, w, freqs, out):
                 scales=w_scales[:, g, cols],
                 in_=w_grouped[:, g, 2 * half : 2 * half + 2, :].rearrange("p c k -> p (c k)"),
             )
+
+        def warm_up(count):
+            for n in range(count):
+                warm = acc_pool.tile([P, BANK], F32, name="acc")
+                nc.tensor.matmul(out=warm[:], lhsT=zeros[:, :P], rhs=zeros[:], start=True, stop=True)
 
         acc_banks = {}
         acc_parts = {}
@@ -290,27 +299,28 @@ def tile_mla_pa_t_kernel(tc, x, w, freqs, out):
 
         rope, nope0, nope1, nope2 = CHUNK_ORDER
         tile_slices = [slice(t, t + 1) for t in range(PAIR)]
+        warm_up(WARM_EARLY)
         transpose_pair(0)
+        warm_up(WARM_LATE)
+        group_w(0, nope2, on_scalar=True)
+        group_w(0, nope0, on_scalar=True)
         group_pair(0)
-        for g in range(PASSES):
-            group_w(g, nope2, on_scalar=True)
-            group_w(g, nope0, on_scalar=True)
+        group_w(1, nope2, on_scalar=True)
+        group_w(1, nope0, on_scalar=True)
         group_w(0, rope, on_scalar=False)
         group_w(0, nope1, on_scalar=False)
-        quantise_pair(0)
         quantise_w_half(0, 1)
         quantise_w_half(0, 0)
-        for half in (1, 0):
-            for t in range(PAIR):
-                multiply_half(0, t, half, (0,))
-        transpose_pair(1)
         group_w(1, rope, on_scalar=False)
-        quantise_w_half(1, 1)
+        quantise_pair(0)
         group_w(1, nope1, on_scalar=False)
+        quantise_w_half(1, 1)
         quantise_w_half(1, 0)
-        for half in (1, 0):
-            for t in range(PAIR):
-                multiply_half(0, t, half, (1,))
+        transpose_pair(1)
+        for g in range(PASSES):
+            for half in (1, 0):
+                for t in range(PAIR):
+                    multiply_half(0, t, half, (g,))
         transpose_pair(2)
         transpose_pair(3)
         group_pair(1)
@@ -324,13 +334,13 @@ def tile_mla_pa_t_kernel(tc, x, w, freqs, out):
         for tile in tile_slices:
             rotate_sum(0, rotate_products(0, tile), tile, engine=nc.gpsimd)
         split_pair(HEAD)
-        quantise_pair(2)
         store(0)
 
         for r in range(1, LAST):
             ahead = r + AHEAD
             if r + HEAD < PAIRS:
                 split_pair(r + HEAD)
+            quantise_pair(r + 1)
             if r % 2 == 0:
                 for n in (ahead, ahead + 1):
                     if n < PAIRS:
@@ -340,10 +350,7 @@ def tile_mla_pa_t_kernel(tc, x, w, freqs, out):
                 group_pair(ahead)
             out_sb = out_pool.tile([P, PAIR * HEADS * QK], F32)
             out_tiles[r] = out_sb
-            terms = rotate_products(r)
-            if ahead < PAIRS:
-                quantise_pair(ahead)
-            rotate_sum(r, terms)
+            rotate_sum(r, rotate_products(r), engine=nc.gpsimd)
             copy_nope(r)
             store(r)
 

@@ -44,7 +44,7 @@ def tile_mla_pa_t_kernel(tc, x, w, freqs, out):
 
     with ExitStack() as ctx:
         const = ctx.enter_context(tc.tile_pool(name="const", bufs=1))
-        x_pool = ctx.enter_context(tc.tile_pool(name="x_pool", bufs=PAIRS))
+        x_pool = ctx.enter_context(tc.tile_pool(name="x_pool", bufs=1))
         perm_pool = ctx.enter_context(tc.tile_pool(name="perm_pool", bufs=3))
         grouped_pool = ctx.enter_context(tc.tile_pool(name="grouped_pool", bufs=3))
         code_pool = ctx.enter_context(tc.tile_pool(name="code_pool", bufs=AHEAD + 2))
@@ -68,17 +68,20 @@ def tile_mla_pa_t_kernel(tc, x, w, freqs, out):
 
         x_tiles = {}
 
-        def load_x(r):
+        def load_x(r, count):
             b, q = divmod(r, PAIRS_PER_BATCH)
-            x_sb = x_pool.tile([P, PAIR * DIM], BF16)
-            nc.sync.dma_start(out=x_sb[:], in_=x_rows[b, :, q * PAIR * DIM : (q + 1) * PAIR * DIM])
-            x_tiles[r] = x_sb
+            width = PAIR * DIM
+            x_sb = x_pool.tile([P, count * width], BF16, name="x%d" % r)
+            nc.sync.dma_start(out=x_sb[:], in_=x_rows[b, :, q * width : (q + count) * width])
+            for n in range(count):
+                x_tiles[r + n] = x_sb[:, n * width : (n + 1) * width]
 
         load_w(0)
-        load_x(0)
+        load_x(0, 1)
         load_w(1)
-        for r in range(1, PAIRS):
-            load_x(r)
+        load_x(1, 1)
+        for r in range(2, PAIRS, 2):
+            load_x(r, 2)
 
         zeros = const.tile([P, BANK], BF16)
         nc.gpsimd.memset(zeros[:], 0.0)
@@ -110,12 +113,12 @@ def tile_mla_pa_t_kernel(tc, x, w, freqs, out):
             split = perm_pool.tile([P, PAIR * DIM], BF16)
             nc.vector.tensor_copy(
                 out=split[:].bitcast(F32).rearrange("p (s u m) -> p s u m", u=2, m=P),
-                in_=x_tiles[r][:].bitcast(F32).rearrange("p (s m u) -> p s u m", u=2, m=P),
+                in_=x_tiles[r].bitcast(F32).rearrange("p (s m u) -> p s u m", u=2, m=P),
             )
             split_tiles[r] = split
 
         def transpose_pair(r):
-            words = (x_tiles[r] if r < HEAD else split_tiles[r])[:].bitcast(F32)
+            words = (x_tiles[r] if r < HEAD else split_tiles[r][:]).bitcast(F32)
             xt_banks[r] = []
             for t in range(PAIR):
                 xt = xt_pool.tile([P, BANK], F32)

@@ -28,10 +28,10 @@ ROPE_CHUNK = CHUNKS - 1
 CHUNK_ORDER = (ROPE_CHUNK, 0, 1, 2)
 BANK = 512
 AHEAD = 2
-LAST = PAIRS - 1
 WARM_EARLY = 7
 WARM_LATE = 6
-TILEWISE = (0, LAST)
+END = PAIRS - 2
+TILEWISE = (0, *range(END, PAIRS))
 HEAD = 4
 
 FLOPS = 2 * BATCH * SEQ * DIM * HEADS * QK
@@ -50,8 +50,8 @@ def tile_mla_pa_t_kernel(tc, x, w, freqs, out):
         code_pool = ctx.enter_context(tc.tile_pool(name="code_pool", bufs=AHEAD + 2))
         term_pool = ctx.enter_context(tc.tile_pool(name="term_pool", bufs=3))
         out_pool = ctx.enter_context(tc.tile_pool(name="out_pool", bufs=6))
-        xt_pool = ctx.enter_context(tc.psum_pool(name="xt_pool", bufs=4))
-        acc_pool = ctx.enter_context(tc.psum_pool(name="acc_pool", bufs=4))
+        xt_pool = ctx.enter_context(tc.psum_pool(name="xt_pool", bufs=3))
+        acc_pool = ctx.enter_context(tc.psum_pool(name="acc_pool", bufs=5))
         ctx.enter_context(tc.manual_schedule())
 
         angles = const.tile([P, TILES * ROPE // 2], BF16)
@@ -203,8 +203,8 @@ def tile_mla_pa_t_kernel(tc, x, w, freqs, out):
                     stop=(g == PASSES - 1),
                 )
 
-        def multiply_pair(r):
-            for c in CHUNK_ORDER:
+        def multiply_pair(r, chunks=CHUNK_ORDER):
+            for c in chunks:
                 acc = acc_pool.tile([P, BANK], F32)
                 acc_banks[r, c] = acc
                 for t in range(PAIR):
@@ -220,10 +220,15 @@ def tile_mla_pa_t_kernel(tc, x, w, freqs, out):
             multiply(acc_banks[r, t, half][:], r, t, slice(half * BANK, (half + 1) * BANK), passes)
 
         def multiply_chunk(r, t, c):
-            xt = xt_pool.tile([P, BANK], F32)
-            acc_parts[r, t, c] = xt
+            if c == ROPE_CHUNK:
+                xt = xt_pool.tile([P, BANK], F32)
+                bank = xt
+            else:
+                acc = acc_pool.tile([P, BANK], F32)
+                bank = acc
+            acc_parts[r, t, c] = bank
             cols = slice(c * CHUNK_COLS, (c + 1) * CHUNK_COLS)
-            multiply(xt[:, :CHUNK_COLS], r, t, cols, range(PASSES))
+            multiply(bank[:, :CHUNK_COLS], r, t, cols, range(PASSES))
 
         def bank_part(r, tiles, c):
             if (r, tiles.start, c) in acc_parts:
@@ -325,7 +330,6 @@ def tile_mla_pa_t_kernel(tc, x, w, freqs, out):
                 for t in range(PAIR):
                     multiply_half(0, t, half, (g,))
         transpose_pair(2)
-        transpose_pair(3)
         group_pair(1)
         quantise_pair(1)
         out_sb = out_pool.tile([P, PAIR * HEADS * QK], F32)
@@ -337,33 +341,40 @@ def tile_mla_pa_t_kernel(tc, x, w, freqs, out):
         for tile in tile_slices:
             rotate_sum(0, rotate_products(0, tile), tile, engine=nc.gpsimd)
         split_pair(HEAD)
+        quantise_pair(2)
         store(0)
 
-        for r in range(1, LAST):
+        for r in range(1, END):
             ahead = r + AHEAD
             if r + HEAD < PAIRS:
                 split_pair(r + HEAD)
-            quantise_pair(r + 1)
-            if r % 2 == 0:
-                for n in (ahead, ahead + 1):
-                    if n < PAIRS:
-                        transpose_pair(n)
-            multiply_pair(r)
+            if r == 1:
+                multiply_pair(r, CHUNK_ORDER[:2])
+                transpose_pair(ahead)
+                multiply_pair(r, CHUNK_ORDER[2:])
+            else:
+                if ahead < PAIRS:
+                    transpose_pair(ahead)
+                multiply_pair(r)
             if ahead < PAIRS:
                 group_pair(ahead)
             out_sb = out_pool.tile([P, PAIR * HEADS * QK], F32)
             out_tiles[r] = out_sb
-            rotate_sum(r, rotate_products(r), engine=nc.gpsimd)
+            terms = rotate_products(r)
+            if ahead < PAIRS:
+                quantise_pair(ahead)
+            rotate_sum(r, terms)
             copy_nope(r)
             store(r)
 
-        out_sb = out_pool.tile([P, PAIR * HEADS * QK], F32)
-        out_tiles[LAST] = out_sb
-        for t, tile in enumerate(tile_slices):
-            multiply_chunk(LAST, t, rope)
-            multiply_chunk(LAST, t, nope2)
-            multiply_half(LAST, t, 0, range(PASSES))
-            rotate_sum(LAST, rotate_products(LAST, tile), tile)
-            copy_chunk2(LAST, t)
-            copy_half0(LAST, t)
-            store(LAST, tile)
+        for r in range(END, PAIRS):
+            out_sb = out_pool.tile([P, PAIR * HEADS * QK], F32)
+            out_tiles[r] = out_sb
+            for t, tile in enumerate(tile_slices):
+                multiply_chunk(r, t, rope)
+                multiply_chunk(r, t, nope2)
+                multiply_half(r, t, 0, range(PASSES))
+                rotate_sum(r, rotate_products(r, tile), tile)
+                copy_chunk2(r, t)
+                copy_half0(r, t)
+                store(r, tile)

from contextlib import ExitStack

import concourse.mybir as mybir
from concourse.masks import make_identity

BF16 = mybir.dt.bfloat16
F32 = mybir.dt.float32
U32 = mybir.dt.uint32
U8 = mybir.dt.uint8
FP8X4 = mybir.dt.float8_e4m3fn_x4
ACT = mybir.ActivationFunctionType
ALU = mybir.AluOpType

P = 128
PACK = 4
BATCH, SEQ, DIM = 4, 1024, 1024
HEADS, NOPE, ROPE = 4, 192, 64
QK = NOPE + ROPE
PASSES = DIM // (P * PACK)
TILES = SEQ // P
PAIR = 2
PAIRS_PER_BATCH = TILES // PAIR
PAIRS = BATCH * PAIRS_PER_BATCH
PART = 64
CHUNKS = QK // PART
CHUNK_COLS = HEADS * PART
ROPE_CHUNK = CHUNKS - 1
CHUNK_ORDER = (ROPE_CHUNK, 0, 1, 2)
BANK = 512
AHEAD = 2
WARM_EARLY = 7
WARM_LATE = 6
END = PAIRS - 2
TILEWISE = (0, *range(END, PAIRS))
HEAD = 4

FLOPS = 2 * BATCH * SEQ * DIM * HEADS * QK


def tile_mla_pa_t_kernel(tc, x, w, freqs, out):
    nc = tc.nc
    x_rows = x.rearrange("b (p i) k -> b p (i k)", i=TILES)
    out_rows = out.rearrange("b (p i) h d -> b p (i h d)", i=TILES)

    with ExitStack() as ctx:
        const = ctx.enter_context(tc.tile_pool(name="const", bufs=1))
        x_pool = ctx.enter_context(tc.tile_pool(name="x_pool", bufs=1))
        perm_pool = ctx.enter_context(tc.tile_pool(name="perm_pool", bufs=3))
        grouped_pool = ctx.enter_context(tc.tile_pool(name="grouped_pool", bufs=3))
        code_pool = ctx.enter_context(tc.tile_pool(name="code_pool", bufs=AHEAD + 2))
        term_pool = ctx.enter_context(tc.tile_pool(name="term_pool", bufs=3))
        out_pool = ctx.enter_context(tc.tile_pool(name="out_pool", bufs=6))
        xt_pool = ctx.enter_context(tc.psum_pool(name="xt_pool", bufs=3))
        acc_pool = ctx.enter_context(tc.psum_pool(name="acc_pool", bufs=5))
        ctx.enter_context(tc.manual_schedule())

        angles = const.tile([P, TILES * ROPE // 2], BF16)
        nc.sync.dma_start(out=angles[:], in_=freqs.rearrange("(p i) j -> p (i j)", i=TILES))

        w_raw = const.tile([P, PASSES, PACK, DIM], BF16)

        def load_w(g):
            rows = w[g * P * PACK : (g + 1) * P * PACK, :]
            nc.sync.dma_start(
                out=w_raw[:, g].rearrange("p t n -> p (t n)"),
                in_=rows.rearrange("(p t) n -> p (t n)", t=PACK),
            )

        x_tiles = {}

        def load_x(r, count):
            b, q = divmod(r, PAIRS_PER_BATCH)
            width = PAIR * DIM
            x_sb = x_pool.tile([P, count * width], BF16, name="x%d" % r)
            nc.sync.dma_start(out=x_sb[:], in_=x_rows[b, :, q * width : (q + count) * width])
            for n in range(count):
                x_tiles[r + n] = x_sb[:, n * width : (n + 1) * width]

        load_w(0)
        load_x(0, 1)
        load_w(1)
        load_x(1, 1)
        for r in range(2, PAIRS, 2):
            load_x(r, 2)

        zeros = const.tile([P, BANK], BF16)
        nc.gpsimd.memset(zeros[:], 0.0)
        ident = const.tile([P, P], F32)
        make_identity(nc, ident[:])

        u_table = const.tile([P, TILES, ROPE], F32)
        v_table = const.tile([P, TILES, ROPE], F32)
        u_cols = u_table[:].rearrange("p i (j e) -> p (i j) e", e=2)
        v_cols = v_table[:].rearrange("p i (j e) -> p (i j) e", e=2)
        half_sin = const.tile([P, TILES * ROPE // 2], F32)
        half_sq = const.tile([P, TILES * ROPE // 2], F32)
        nc.scalar.activation(out=half_sin[:], in_=angles[:], func=ACT.Sin, scale=0.5)
        nc.scalar.activation(out=u_cols[:, :, 1], in_=angles[:], func=ACT.Sin)
        nc.scalar.activation(out=v_cols[:, :, 0], in_=angles[:], func=ACT.Sin, scale=-1.0)
        nc.vector.tensor_tensor(out=half_sq[:], in0=half_sin[:], in1=half_sin[:], op=ALU.mult)
        for cos_cols in (u_cols[:, :, 0], v_cols[:, :, 1]):
            nc.vector.tensor_scalar(
                out=cos_cols, in0=half_sq[:], scalar1=-2.0, scalar2=1.0, op0=ALU.mult, op1=ALU.add
            )

        split_tiles = {}
        xt_banks = {}
        grouped_tiles = {}
        x_codes = {}
        x_scales = {}

        def split_pair(r):
            split = perm_pool.tile([P, PAIR * DIM], BF16)
            nc.vector.tensor_copy(
                out=split[:].bitcast(F32).rearrange("p (s u m) -> p s u m", u=2, m=P),
                in_=x_tiles[r].bitcast(F32).rearrange("p (s m u) -> p s u m", u=2, m=P),
            )
            split_tiles[r] = split

        def transpose_pair(r):
            words = (x_tiles[r] if r < HEAD else split_tiles[r][:]).bitcast(F32)
            xt_banks[r] = []
            for t in range(PAIR):
                xt = xt_pool.tile([P, BANK], F32)
                for s in range(PACK):
                    g, u = divmod(s, 2)
                    if r < HEAD:
                        first = t * BANK + g * 2 * P
                        cols = slice(first + u, first + 2 * P, 2)
                    else:
                        first = (t * PACK + s) * P
                        cols = slice(first, first + P)
                    nc.tensor.transpose(
                        out=xt[:, s * P : (s + 1) * P], in_=words[:, cols], identity=ident[:]
                    )
                xt_banks[r].append(xt)

        def group_pair(r):
            grouped = grouped_pool.tile([P, PAIR * DIM], BF16, align_bytes=64)
            grouped_words = grouped[:].bitcast(F32)
            for t in range(PAIR):
                nc.scalar.copy(
                    out=grouped_words[:, t * BANK : (t + 1) * BANK].rearrange(
                        "p (g k u) -> p g k u", g=PASSES, u=2
                    ),
                    in_=xt_banks[r][t][:].rearrange("p (g u k) -> p g k u", g=PASSES, u=2),
                )
            grouped_tiles[r] = grouped

        def quantise_pair(r):
            codes = code_pool.tile([P, PAIR * PASSES * P], U32, align_bytes=64)
            scales = code_pool.tile([P, PAIR * PASSES * P], U8, align_bytes=64)
            nc.vector.quantize_mx(
                out=codes[:].bitcast(FP8X4), scales=scales[:], in_=grouped_tiles[r][:]
            )
            x_codes[r] = codes
            x_scales[r] = scales

        w_grouped = const.tile([P, PASSES, CHUNKS, CHUNK_COLS * PACK], BF16, align_bytes=64)
        w_codes = const.tile([P, PASSES, CHUNKS * CHUNK_COLS], U32, align_bytes=64)
        w_scales = const.tile([P, PASSES, CHUNKS * CHUNK_COLS], U8, align_bytes=64)

        def group_w(g, c, on_scalar):
            if c == ROPE_CHUNK:
                src = w_raw[:, g, :, HEADS * NOPE :].rearrange("p t (h n) -> p h n t", h=HEADS)
            else:
                src = w_raw[:, g, :, : HEADS * NOPE].rearrange(
                    "p t (h c n) -> p c h n t", h=HEADS, n=PART
                )[:, c]
            dst = w_grouped[:, g, c, :].rearrange("p (h n t) -> p h n t", h=HEADS, t=PACK)
            if on_scalar:
                nc.scalar.copy(out=dst, in_=src)
            else:
                nc.vector.tensor_copy(out=dst, in_=src)

        def quantise_w_half(g, half):
            cols = slice(half * BANK, (half + 1) * BANK)
            nc.vector.quantize_mx(
                out=w_codes[:, g, cols].bitcast(FP8X4),
                scales=w_scales[:, g, cols],
                in_=w_grouped[:, g, 2 * half : 2 * half + 2, :].rearrange("p c k -> p (c k)"),
            )

        def warm_up(count):
            for n in range(count):
                warm = acc_pool.tile([P, BANK], F32, name="acc")
                nc.tensor.matmul(out=warm[:], lhsT=zeros[:, :P], rhs=zeros[:], start=True, stop=True)

        acc_banks = {}
        acc_parts = {}
        out_tiles = {}

        def multiply(acc_cols, r, t, w_cols, passes):
            for g in passes:
                x_cols = slice((t * PASSES + g) * P, (t * PASSES + g + 1) * P)
                nc.tensor.matmul_mx(
                    out=acc_cols,
                    lhsT=x_codes[r][:, x_cols].bitcast(FP8X4),
                    lhsT_scale=x_scales[r][:, x_cols],
                    rhs=w_codes[:, g, w_cols].bitcast(FP8X4),
                    rhs_scale=w_scales[:, g, w_cols],
                    start=(g == 0),
                    stop=(g == PASSES - 1),
                )

        def multiply_pair(r, chunks=CHUNK_ORDER):
            for c in chunks:
                acc = acc_pool.tile([P, BANK], F32)
                acc_banks[r, c] = acc
                for t in range(PAIR):
                    multiply(
                        acc[:, t * CHUNK_COLS : (t + 1) * CHUNK_COLS],
                        r, t, slice(c * CHUNK_COLS, (c + 1) * CHUNK_COLS), range(PASSES),
                    )

        def multiply_half(r, t, half, passes):
            if 0 in passes:
                acc = acc_pool.tile([P, BANK], F32)
                acc_banks[r, t, half] = acc
            multiply(acc_banks[r, t, half][:], r, t, slice(half * BANK, (half + 1) * BANK), passes)

        def multiply_chunk(r, t, c):
            if c == ROPE_CHUNK:
                xt = xt_pool.tile([P, BANK], F32)
                bank = xt
            else:
                acc = acc_pool.tile([P, BANK], F32)
                bank = acc
            acc_parts[r, t, c] = bank
            cols = slice(c * CHUNK_COLS, (c + 1) * CHUNK_COLS)
            multiply(bank[:, :CHUNK_COLS], r, t, cols, range(PASSES))

        def bank_part(r, tiles, c):
            if (r, tiles.start, c) in acc_parts:
                return acc_parts[r, tiles.start, c][:, :CHUNK_COLS]
            if r in TILEWISE:
                half, side = divmod(c, 2)
                return acc_banks[r, tiles.start, half][:, side * CHUNK_COLS : (side + 1) * CHUNK_COLS]
            return acc_banks[r, c][:]

        split = "p (t h j e) -> p t h j e"
        by_head = "p (t h n) -> p t h n"
        both = slice(0, PAIR)

        def rotate_products(r, tiles=both):
            count = tiles.stop - tiles.start
            full = [P, count, HEADS, ROPE // 2, 2]
            i0 = (r % PAIRS_PER_BATCH) * PAIR + tiles.start
            pairs = bank_part(r, tiles, ROPE_CHUNK).rearrange(split, t=count, h=HEADS, e=2)
            terms = []
            for e, table in enumerate((u_table, v_table)):
                term = term_pool.tile([P, BANK], F32, name="term%d" % e)
                nc.vector.tensor_tensor(
                    out=term[:, : count * CHUNK_COLS].rearrange(split, t=count, h=HEADS, e=2),
                    in0=pairs[:, :, :, :, e : e + 1].to_broadcast(full),
                    in1=table[:, i0 : i0 + count, :]
                    .rearrange("p t (j e) -> p t j e", e=2)
                    .unsqueeze(2)
                    .to_broadcast(full),
                    op=ALU.mult,
                )
                terms.append(term)
            return terms

        def out_view(r, tiles):
            return out_tiles[r][:].rearrange("p (t h d) -> p t h d", t=PAIR, h=HEADS)[:, tiles]

        def out_part(r, tiles, c):
            return out_view(r, tiles)[:, :, :, c * PART : (c + 1) * PART]

        def rotate_sum(r, terms, tiles=both, engine=nc.vector):
            count = tiles.stop - tiles.start
            in0, in1 = (
                term[:, : count * CHUNK_COLS].rearrange(by_head, t=count, h=HEADS) for term in terms
            )
            engine.tensor_tensor(out=out_part(r, tiles, ROPE_CHUNK), in0=in0, in1=in1, op=ALU.add)

        def copy_nope(r):
            for c in range(ROPE_CHUNK):
                nc.scalar.copy(
                    out=out_part(r, both, c),
                    in_=bank_part(r, both, c).rearrange(by_head, t=PAIR, h=HEADS),
                )

        def copy_half0(r, t):
            nc.scalar.copy(
                out=out_view(r, slice(t, t + 1))[:, 0, :, : 2 * PART].rearrange(
                    "p h (c n) -> p c h n", c=2
                ),
                in_=acc_banks[r, t, 0][:].rearrange("p (c h n) -> p c h n", c=2, h=HEADS),
            )

        def copy_chunk2(r, t):
            tile = slice(t, t + 1)
            nc.scalar.copy(
                out=out_part(r, tile, 2),
                in_=bank_part(r, tile, 2).rearrange(by_head, t=1, h=HEADS),
            )

        def store(r, tiles=both):
            b, q = divmod(r, PAIRS_PER_BATCH)
            width = HEADS * QK
            nc.sync.dma_start(
                out=out_rows[b, :, (q * PAIR + tiles.start) * width : (q * PAIR + tiles.stop) * width],
                in_=out_tiles[r][:, tiles.start * width : tiles.stop * width],
            )

        rope, nope0, nope1, nope2 = CHUNK_ORDER
        tile_slices = [slice(t, t + 1) for t in range(PAIR)]
        warm_up(WARM_EARLY)
        transpose_pair(0)
        warm_up(WARM_LATE)
        group_w(0, nope2, on_scalar=True)
        group_w(0, nope0, on_scalar=True)
        group_pair(0)
        group_w(1, nope2, on_scalar=True)
        group_w(1, nope0, on_scalar=True)
        group_w(0, rope, on_scalar=False)
        group_w(0, nope1, on_scalar=False)
        quantise_w_half(0, 1)
        quantise_w_half(0, 0)
        group_w(1, rope, on_scalar=False)
        quantise_pair(0)
        group_w(1, nope1, on_scalar=False)
        quantise_w_half(1, 1)
        quantise_w_half(1, 0)
        transpose_pair(1)
        for g in range(PASSES):
            for half in (1, 0):
                for t in range(PAIR):
                    multiply_half(0, t, half, (g,))
        transpose_pair(2)
        group_pair(1)
        quantise_pair(1)
        out_sb = out_pool.tile([P, PAIR * HEADS * QK], F32)
        out_tiles[0] = out_sb
        for t in range(PAIR):
            copy_chunk2(0, t)
            copy_half0(0, t)
        group_pair(2)
        for tile in tile_slices:
            rotate_sum(0, rotate_products(0, tile), tile, engine=nc.gpsimd)
        split_pair(HEAD)
        quantise_pair(2)
        store(0)

        for r in range(1, END):
            ahead = r + AHEAD
            if r + HEAD < PAIRS:
                split_pair(r + HEAD)
            if r == 1:
                multiply_pair(r, CHUNK_ORDER[:2])
                transpose_pair(ahead)
                multiply_pair(r, CHUNK_ORDER[2:])
            else:
                if ahead < PAIRS:
                    transpose_pair(ahead)
                multiply_pair(r)
            if ahead < PAIRS:
                group_pair(ahead)
            out_sb = out_pool.tile([P, PAIR * HEADS * QK], F32)
            out_tiles[r] = out_sb
            terms = rotate_products(r)
            if ahead < PAIRS:
                quantise_pair(ahead)
            rotate_sum(r, terms)
            copy_nope(r)
            store(r)

        for r in range(END, PAIRS):
            out_sb = out_pool.tile([P, PAIR * HEADS * QK], F32)
            out_tiles[r] = out_sb
            for t, tile in enumerate(tile_slices):
                multiply_chunk(r, t, rope)
                multiply_chunk(r, t, nope2)
                multiply_half(r, t, 0, range(PASSES))
                rotate_sum(r, rotate_products(r, tile), tile)
                copy_chunk2(r, t)
                copy_half0(r, t)
                store(r, tile)
